import numpy as np
import ml_dtypes


def mxq(x, axis, fmt="e4m3"):
    dtype, down = {"e4m3": (ml_dtypes.float8_e4m3fn, 7), "e5m2": (ml_dtypes.float8_e5m2, 14)}[fmt]
    v = np.moveaxis(np.asarray(x, np.float32).astype(ml_dtypes.bfloat16).astype(np.float64), axis, -1)
    blocks = v.reshape(v.shape[:-1] + (-1, 32))
    amax = np.abs(blocks).max(-1, keepdims=True)
    byte = np.maximum(np.where(amax > 0, np.frexp(amax)[1] - 1 + 127, 0) - down, 1)
    scale = np.exp2(byte - 127.0)
    codes = (blocks / scale).astype(np.float32).astype(dtype).astype(np.float64)
    return np.moveaxis((codes * scale).reshape(v.shape), -1, axis)


WIDE = False


def mx_kscale(k):
    if not WIDE:
        return np.ones(k)
    levels = np.array([10, -10, 5, -5, 0])
    a = np.random.permutation(np.resize(levels, k // 512 * 4)).reshape(k // 512, 4)
    idx = np.arange(k)
    return np.exp2(a[idx // 512, idx % 128 // 32])


BF16 = ml_dtypes.bfloat16


def bf(x):
    return np.asarray(x, np.float32).astype(BF16)


def f64(x):
    return np.asarray(x).astype(np.float64)


E2M1 = np.array([0.0, 0.5, 1.0, 1.5, 2.0, 3.0, 4.0, 6.0, -0.0, -0.5, -1.0, -1.5, -2.0, -3.0, -4.0, -6.0])


def pack_weight(w, fmt):
    k, n = w.shape
    w = f64(bf(w)).reshape(k // 32, 32, n)
    amax = np.abs(w).max(1)
    if fmt == "e4m3":
        byte = np.frexp(amax)[1] - 1 + 127 - 7
    else:
        mant, ex = np.frexp(amax / 6.0)
        byte = np.where(mant > 0.5, ex, ex - 1) + 127
    byte = np.clip(np.where(amax > 0, byte, 1), 1, 254)
    scaled = (w * np.exp2(127.0 - byte)[:, None, :]).reshape(k, n).astype(np.float32)
    by_word = np.ascontiguousarray(scaled.reshape(k // 512, 128, 4, n).transpose(0, 1, 3, 2))
    if fmt == "e4m3":
        words = by_word.astype(ml_dtypes.float8_e4m3fn).view(np.uint8)
    else:
        c = by_word.astype(ml_dtypes.float4_e2m1fn).view(np.uint8) & 0xF
        words = c[..., 0::2] | (c[..., 1::2] << 4)
    return np.ascontiguousarray(words), np.ascontiguousarray(byte.astype(np.uint8).reshape(k // 512, 16, n))


def unpack_weight(words, scales, fmt):
    g, p, n, _ = words.shape
    if fmt == "e4m3":
        vals = np.ascontiguousarray(words).view(ml_dtypes.float8_e4m3fn).astype(np.float64)
    else:
        nib = np.empty((g, p, n, 4), np.uint8)
        nib[..., 0::2] = words & 0xF
        nib[..., 1::2] = words >> 4
        vals = E2M1[nib]
    vals = vals * np.repeat(np.exp2(scales.astype(np.float64) - 127.0), 8, axis=1)[..., None]
    return vals.transpose(0, 1, 3, 2).reshape(g * 512, n)

def pack4(w):
    words, scales = pack_weight(w, "e2m1")
    return words.reshape(words.shape[0], 128, -1), scales


def unpack4(words, scales):
    return unpack_weight(words.reshape(words.shape[0], 128, -1, 2), scales, "e2m1")


B, S, H, R = 2, 512, 4096, 1024
G = H // R


def setup_inputs():
    s = mx_kscale(R)
    x = bf(np.random.standard_normal((B, S, H)) * np.tile(s, G))
    words, scales = pack4(np.random.standard_normal((R, R)) / np.sqrt(R) / s[:, None])
    return {"x": x, "matrix_words": words, "matrix_scales": scales}


def reference(x, matrix_words, matrix_scales):
    x = f64(x)
    matrix = unpack4(matrix_words, matrix_scales)
    b, n, h = x.shape
    r = matrix.shape[0]
    g = h // r
    compressed = x.reshape(b, n, g, r).sum(axis=2)
    out = mxq(compressed, 2, "e4m3") @ matrix
    return np.repeat(out, g, axis=2)[:, :, :h]

@@ -1,0 +1,149 @@
+from contextlib import ExitStack
+
+import concourse.mybir as mybir
+from concourse.masks import make_identity
+
+BF16 = mybir.dt.bfloat16
+F32 = mybir.dt.float32
+I32 = mybir.dt.int32
+U32 = mybir.dt.uint32
+U8 = mybir.dt.uint8
+FP8X4 = mybir.dt.float8_e4m3fn_x4
+FP4X4 = mybir.dt.float4_e2m1fn_x4
+
+P = 128
+PACK = 4
+K_PASS = P * PACK
+TOKENS = 2 * 512
+HIDDEN = 4096
+RANK = 1024
+GROUPS = HIDDEN // RANK
+PASSES = RANK // K_PASS
+N_TILE = 512
+N_TILES = RANK // N_TILE
+TOKEN_TILES = TOKENS // P
+OUT_BUFS = 6
+VECTOR_HELPS = 2
+
+FLOPS = 2 * TOKENS * RANK * RANK
+
+
+def tile_mora_kernel(tc, x, matrix_words, matrix_scales, out):
+    nc = tc.nc
+    x_tiles = x.flatten_outer_dims().rearrange("(p i) h -> p i h", i=TOKEN_TILES)
+    out_tiles = out.flatten_outer_dims().rearrange("(p i) h -> p i h", i=TOKEN_TILES)
+
+    with ExitStack() as ctx:
+        keep = ctx.enter_context(tc.tile_pool(name="keep", bufs=1))
+        work = ctx.enter_context(tc.tile_pool(name="work", bufs=2))
+        results = ctx.enter_context(tc.tile_pool(name="results", bufs=OUT_BUFS))
+        psum_t = ctx.enter_context(tc.psum_pool(name="psum_t", bufs=2))
+        psum_y = ctx.enter_context(tc.psum_pool(name="psum_y", bufs=4))
+        ctx.enter_context(tc.manual_schedule())
+
+        w_words = keep.tile([P, PASSES, 2 * RANK], U8, align_bytes=64)
+        w_scales = keep.tile([P, PASSES, RANK], U8, align_bytes=64)
+        identity = keep.tile([P, P], BF16)
+        x_sb = [keep.tile([P, HIDDEN], BF16, name="x_sb%d" % i) for i in range(TOKEN_TILES)]
+
+        nc.vector.memset(w_scales[:].bitcast(I32), 0)
+        make_identity(nc, identity[:])
+
+        nc.sync.dma_start(out=x_sb[0][:], in_=x_tiles[:, 0, :])
+        for quadrant in range(4):
+            nc.sync.dma_start(
+                out=w_scales[32 * quadrant : 32 * quadrant + 4, :, :].bitcast(I32),
+                in_=matrix_scales[:, 4 * quadrant : 4 * quadrant + 4, :].bitcast(I32).rearrange("g r w -> r g w"),
+            )
+        nc.sync.dma_start(
+            out=w_words[:].bitcast(I32),
+            in_=matrix_words.bitcast(I32).rearrange("g p w -> p g w"),
+        )
+        for i in range(1, TOKEN_TILES):
+            nc.sync.dma_start(out=x_sb[i][:], in_=x_tiles[:, i, :])
+
+        turned = {}
+
+        def pair_sums(i):
+            pairs = work.tile([P, 2 * RANK], F32, name="pairs")
+            nc.vector.tensor_tensor(
+                out=pairs[:], in0=x_sb[i][:, : 2 * RANK], in1=x_sb[i][:, 2 * RANK :], op=mybir.AluOpType.add
+            )
+            return pairs
+
+        def finish_sum_and_transpose(i, pairs):
+            c = work.tile([P, RANK], BF16, name="c")
+            nc.vector.tensor_tensor(out=c[:], in0=pairs[:, :RANK], in1=pairs[:, RANK:], op=mybir.AluOpType.add)
+            c_t = psum_t.tile([P, PASSES * PACK, P], BF16, name="c_t")
+            for g in range(PASSES):
+                for t in range(PACK):
+                    nc.tensor.transpose(
+                        c_t[:, g * PACK + t, :], c[:, K_PASS * g + t : K_PASS * (g + 1) : PACK], identity[:]
+                    )
+            turned[i] = c_t
+
+        def regroup(i):
+            grouped = work.tile([P, PASSES, P, PACK], BF16, name="grouped", align_bytes=64)
+            nc.vector.tensor_copy(out=grouped[:], in_=turned[i][:].rearrange("p (g t) r -> p g r t", g=PASSES))
+            return grouped
+
+        def repeated(y):
+            return y[:].unsqueeze(2).to_broadcast([P, N_TILE, GROUPS])
+
+        def store(i, result, first_n, n_count):
+            first = N_TILE * first_n
+            last = N_TILE * (first_n + n_count)
+            nc.sync.dma_start(
+                out=out_tiles[:, i, GROUPS * first : GROUPS * last],
+                in_=result[:, first:last, :].rearrange("p n j -> p (n j)"),
+            )
+
+        left_to_vector = {}
+
+        def multiply(i, grouped):
+            c_codes = work.tile([P, PASSES * P], U32, name="c_codes", align_bytes=64)
+            c_scales = work.tile([P, PASSES * P], U8, name="c_scales", align_bytes=64)
+            nc.vector.quantize_mx(
+                out=c_codes[:].bitcast(FP8X4),
+                scales=c_scales[:],
+                in_=grouped[:].rearrange("p g r t -> p (g r t)"),
+            )
+            halves = []
+            for n in range(N_TILES):
+                y = psum_y.tile([P, N_TILE], F32, name="y")
+                for g in range(PASSES):
+                    nc.tensor.matmul_mx(
+                        out=y[:],
+                        lhsT=c_codes[:, g * P : (g + 1) * P].bitcast(FP8X4),
+                        lhsT_scale=c_scales[:, g * P : (g + 1) * P],
+                        rhs=w_words[:, g, 2 * N_TILE * n : 2 * N_TILE * (n + 1)].bitcast(FP4X4),
+                        rhs_scale=w_scales[:, g, N_TILE * n : N_TILE * (n + 1)],
+                        start=(g == 0),
+                        stop=(g == PASSES - 1),
+                    )
+                halves.append(y)
+            result = results.tile([P, RANK, GROUPS], F32, name="result")
+            nc.scalar.copy(out=result[:, :N_TILE, :], in_=repeated(halves[0]))
+            if i < TOKEN_TILES - VECTOR_HELPS:
+                nc.scalar.copy(out=result[:, N_TILE:, :], in_=repeated(halves[1]))
+                store(i, result, 0, N_TILES)
+            else:
+                store(i, result, 0, 1)
+                left_to_vector[i] = (halves[1], result)
+
+        def vector_helps(i):
+            y, result = left_to_vector[i]
+            nc.vector.tensor_copy(out=result[:, N_TILE:, :], in_=repeated(y))
+            store(i, result, 1, 1)
+
+        for i in range(TOKEN_TILES + 2):
+            if i < TOKEN_TILES:
+                pairs = pair_sums(i)
+            if 1 <= i <= TOKEN_TILES:
+                grouped = regroup(i - 1)
+            if i < TOKEN_TILES:
+                finish_sum_and_transpose(i, pairs)
+            if 1 <= i <= TOKEN_TILES:
+                multiply(i - 1, grouped)
+            if i - 2 in left_to_vector:
+                vector_helps(i - 2)

@@ -22,7 +22,7 @@ PASSES = RANK // K_PASS
 N_TILE = 512
 N_TILES = RANK // N_TILE
 TOKEN_TILES = TOKENS // P
-OUT_BUFS = 6
+OUT_BUFS = 12
 VECTOR_HELPS = 2
 
 FLOPS = 2 * TOKENS * RANK * RANK
@@ -90,12 +90,10 @@ def tile_mora_kernel(tc, x, matrix_words, matrix_scales, out):
         def repeated(y):
             return y[:].unsqueeze(2).to_broadcast([P, N_TILE, GROUPS])
 
-        def store(i, result, first_n, n_count):
-            first = N_TILE * first_n
-            last = N_TILE * (first_n + n_count)
+        def store(i, n, result):
             nc.sync.dma_start(
-                out=out_tiles[:, i, GROUPS * first : GROUPS * last],
-                in_=result[:, first:last, :].rearrange("p n j -> p (n j)"),
+                out=out_tiles[:, i, GROUPS * N_TILE * n : GROUPS * N_TILE * (n + 1)],
+                in_=result[:].rearrange("p n j -> p (n j)"),
             )
 
         left_to_vector = {}
@@ -108,7 +106,6 @@ def tile_mora_kernel(tc, x, matrix_words, matrix_scales, out):
                 scales=c_scales[:],
                 in_=grouped[:].rearrange("p g r t -> p (g r t)"),
             )
-            halves = []
             for n in range(N_TILES):
                 y = psum_y.tile([P, N_TILE], F32, name="y")
                 for g in range(PASSES):
@@ -121,20 +118,17 @@ def tile_mora_kernel(tc, x, matrix_words, matrix_scales, out):
                         start=(g == 0),
                         stop=(g == PASSES - 1),
                     )
-                halves.append(y)
-            result = results.tile([P, RANK, GROUPS], F32, name="result")
-            nc.scalar.copy(out=result[:, :N_TILE, :], in_=repeated(halves[0]))
-            if i < TOKEN_TILES - VECTOR_HELPS:
-                nc.scalar.copy(out=result[:, N_TILE:, :], in_=repeated(halves[1]))
-                store(i, result, 0, N_TILES)
-            else:
-                store(i, result, 0, 1)
-                left_to_vector[i] = (halves[1], result)
+                if n == N_TILES - 1 and i >= TOKEN_TILES - VECTOR_HELPS:
+                    left_to_vector[i] = y
+                else:
+                    result = results.tile([P, N_TILE, GROUPS], F32, name="result")
+                    nc.scalar.copy(out=result[:], in_=repeated(y))
+                    store(i, n, result)
 
         def vector_helps(i):
-            y, result = left_to_vector[i]
-            nc.vector.tensor_copy(out=result[:, N_TILE:, :], in_=repeated(y))
-            store(i, result, 1, 1)
+            result = results.tile([P, N_TILE, GROUPS], F32, name="result")
+            nc.vector.tensor_copy(out=result[:], in_=repeated(left_to_vector[i]))
+            store(i, N_TILES - 1, result)
 
         for i in range(TOKEN_TILES + 2):
             if i < TOKEN_TILES:

@@ -13,6 +13,7 @@ FP4X4 = mybir.dt.float4_e2m1fn_x4
 
 P = 128
 PACK = 4
+HALVES = 2
 K_PASS = P * PACK
 TOKENS = 2 * 512
 HIDDEN = 4096
@@ -43,7 +44,7 @@ def tile_mora_kernel(tc, x, matrix_words, matrix_scales, out):
 
         w_words = keep.tile([P, PASSES, 2 * RANK], U8, align_bytes=64)
         w_scales = keep.tile([P, PASSES, RANK], U8, align_bytes=64)
-        identity = keep.tile([P, P], BF16)
+        identity = keep.tile([P, P], F32)
         x_sb = [keep.tile([P, HIDDEN], BF16, name="x_sb%d" % i) for i in range(TOKEN_TILES)]
 
         nc.vector.memset(w_scales[:].bitcast(I32), 0)
@@ -74,17 +75,23 @@ def tile_mora_kernel(tc, x, matrix_words, matrix_scales, out):
         def finish_sum_and_transpose(i, pairs):
             c = work.tile([P, RANK], BF16, name="c")
             nc.vector.tensor_tensor(out=c[:], in0=pairs[:, :RANK], in1=pairs[:, RANK:], op=mybir.AluOpType.add)
-            c_t = psum_t.tile([P, PASSES * PACK, P], BF16, name="c_t")
+            words = c[:].bitcast(F32)
+            c_t = psum_t.tile([P, PASSES * HALVES, P], F32, name="c_t")
             for g in range(PASSES):
-                for t in range(PACK):
+                for u in range(HALVES):
                     nc.tensor.transpose(
-                        c_t[:, g * PACK + t, :], c[:, K_PASS * g + t : K_PASS * (g + 1) : PACK], identity[:]
+                        c_t[:, g * HALVES + u, :],
+                        words[:, K_PASS // 2 * g + u : K_PASS // 2 * (g + 1) : HALVES],
+                        identity[:],
                     )
             turned[i] = c_t
 
         def regroup(i):
             grouped = work.tile([P, PASSES, P, PACK], BF16, name="grouped", align_bytes=64)
-            nc.vector.tensor_copy(out=grouped[:], in_=turned[i][:].rearrange("p (g t) r -> p g r t", g=PASSES))
+            nc.vector.tensor_copy(
+                out=grouped[:].rearrange("p g r t -> p (g r t)").bitcast(F32).rearrange("p (g r u) -> p g r u", g=PASSES, u=HALVES),
+                in_=turned[i][:].rearrange("p (g u) r -> p g r u", g=PASSES),
+            )
             return grouped
 
         def repeated(y):

@@ -23,7 +23,8 @@ PASSES = RANK // K_PASS
 N_TILE = 512
 N_TILES = RANK // N_TILE
 TOKEN_TILES = TOKENS // P
-OUT_BUFS = 12
+LOAD_GROUPS = (1, 1, 2, 4)
+STORE_GROUPS = (2, 2, 2, 2, 2, 2, 4)
 VECTOR_HELPS = 2
 
 FLOPS = 2 * TOKENS * RANK * RANK
@@ -31,13 +32,13 @@ FLOPS = 2 * TOKENS * RANK * RANK
 
 def tile_mora_kernel(tc, x, matrix_words, matrix_scales, out):
     nc = tc.nc
-    x_tiles = x.flatten_outer_dims().rearrange("(p i) h -> p i h", i=TOKEN_TILES)
-    out_tiles = out.flatten_outer_dims().rearrange("(p i) h -> p i h", i=TOKEN_TILES)
+    x_rows = x.flatten_outer_dims().rearrange("(p i) h -> p (i h)", i=TOKEN_TILES)
+    out_rows = out.flatten_outer_dims().rearrange("(p i) h -> p (i h)", i=TOKEN_TILES)
 
     with ExitStack() as ctx:
         keep = ctx.enter_context(tc.tile_pool(name="keep", bufs=1))
         work = ctx.enter_context(tc.tile_pool(name="work", bufs=2))
-        results = ctx.enter_context(tc.tile_pool(name="results", bufs=OUT_BUFS))
+        results = ctx.enter_context(tc.tile_pool(name="results", bufs=1))
         psum_t = ctx.enter_context(tc.psum_pool(name="psum_t", bufs=2))
         psum_y = ctx.enter_context(tc.psum_pool(name="psum_y", bufs=4))
         ctx.enter_context(tc.manual_schedule())
@@ -45,12 +46,27 @@ def tile_mora_kernel(tc, x, matrix_words, matrix_scales, out):
         w_words = keep.tile([P, PASSES, 2 * RANK], U8, align_bytes=64)
         w_scales = keep.tile([P, PASSES, RANK], U8, align_bytes=64)
         identity = keep.tile([P, P], F32)
-        x_sb = [keep.tile([P, HIDDEN], BF16, name="x_sb%d" % i) for i in range(TOKEN_TILES)]
+        x_loads = [keep.tile([P, count * HIDDEN], BF16, name="x_load%d" % j) for j, count in enumerate(LOAD_GROUPS)]
+        x_sb = []
+        for j, count in enumerate(LOAD_GROUPS):
+            for m in range(count):
+                x_sb.append(x_loads[j][:, m * HIDDEN : (m + 1) * HIDDEN])
+        HALF = GROUPS * N_TILE
+        out_sb = [results.tile([P, count * HALF], F32, name="out_sb%d" % j) for j, count in enumerate(STORE_GROUPS)]
+        place = []
+        for j, count in enumerate(STORE_GROUPS):
+            for m in range(count):
+                place.append((j, m))
+        written = [0 for count in STORE_GROUPS]
 
         nc.vector.memset(w_scales[:].bitcast(I32), 0)
         make_identity(nc, identity[:])
 
-        nc.sync.dma_start(out=x_sb[0][:], in_=x_tiles[:, 0, :])
+        def load(j):
+            first = sum(LOAD_GROUPS[:j])
+            nc.sync.dma_start(out=x_loads[j][:], in_=x_rows[:, first * HIDDEN : (first + LOAD_GROUPS[j]) * HIDDEN])
+
+        load(0)
         for quadrant in range(4):
             nc.sync.dma_start(
                 out=w_scales[32 * quadrant : 32 * quadrant + 4, :, :].bitcast(I32),
@@ -60,8 +76,8 @@ def tile_mora_kernel(tc, x, matrix_words, matrix_scales, out):
             out=w_words[:].bitcast(I32),
             in_=matrix_words.bitcast(I32).rearrange("g p w -> p g w"),
         )
-        for i in range(1, TOKEN_TILES):
-            nc.sync.dma_start(out=x_sb[i][:], in_=x_tiles[:, i, :])
+        for j in range(1, len(LOAD_GROUPS)):
+            load(j)
 
         turned = {}
 
@@ -97,11 +113,16 @@ def tile_mora_kernel(tc, x, matrix_words, matrix_scales, out):
         def repeated(y):
             return y[:].unsqueeze(2).to_broadcast([P, N_TILE, GROUPS])
 
-        def store(i, n, result):
-            nc.sync.dma_start(
-                out=out_tiles[:, i, GROUPS * N_TILE * n : GROUPS * N_TILE * (n + 1)],
-                in_=result[:].rearrange("p n j -> p (n j)"),
-            )
+        def target(i, n):
+            j, m = place[N_TILES * i + n]
+            return out_sb[j][:, m * HALF : (m + 1) * HALF].rearrange("p (n j) -> p n j", j=GROUPS)
+
+        def store_if_full(i, n):
+            j, m = place[N_TILES * i + n]
+            written[j] += 1
+            if written[j] == STORE_GROUPS[j]:
+                first = sum(STORE_GROUPS[:j])
+                nc.sync.dma_start(out=out_rows[:, first * HALF : (first + STORE_GROUPS[j]) * HALF], in_=out_sb[j][:])
 
         left_to_vector = {}
 
@@ -128,14 +149,12 @@ def tile_mora_kernel(tc, x, matrix_words, matrix_scales, out):
                 if n == N_TILES - 1 and i >= TOKEN_TILES - VECTOR_HELPS:
                     left_to_vector[i] = y
                 else:
-                    result = results.tile([P, N_TILE, GROUPS], F32, name="result")
-                    nc.scalar.copy(out=result[:], in_=repeated(y))
-                    store(i, n, result)
+                    nc.scalar.copy(out=target(i, n), in_=repeated(y))
+                    store_if_full(i, n)
 
         def vector_helps(i):
-            result = results.tile([P, N_TILE, GROUPS], F32, name="result")
-            nc.vector.tensor_copy(out=result[:], in_=repeated(left_to_vector[i]))
-            store(i, N_TILES - 1, result)
+            nc.vector.tensor_copy(out=target(i, N_TILES - 1), in_=repeated(left_to_vector[i]))
+            store_if_full(i, N_TILES - 1)
 
         for i in range(TOKEN_TILES + 2):
             if i < TOKEN_TILES:

@@ -67,6 +67,7 @@ def tile_mora_kernel(tc, x, matrix_words, matrix_scales, out):
             nc.sync.dma_start(out=x_loads[j][:], in_=x_rows[:, first * HIDDEN : (first + LOAD_GROUPS[j]) * HIDDEN])
 
         load(0)
+        load(1)
         for quadrant in range(4):
             nc.sync.dma_start(
                 out=w_scales[32 * quadrant : 32 * quadrant + 4, :, :].bitcast(I32),
@@ -76,7 +77,7 @@ def tile_mora_kernel(tc, x, matrix_words, matrix_scales, out):
             out=w_words[:].bitcast(I32),
             in_=matrix_words.bitcast(I32).rearrange("g p w -> p g w"),
         )
-        for j in range(1, len(LOAD_GROUPS)):
+        for j in range(2, len(LOAD_GROUPS)):
             load(j)
 
         turned = {}

@@ -23,7 +23,8 @@ PASSES = RANK // K_PASS
 N_TILE = 512
 N_TILES = RANK // N_TILE
 TOKEN_TILES = TOKENS // P
-LOAD_GROUPS = (1, 1, 2, 4)
+LOAD_GROUPS = (1, 1, 1, 1, 2, 2)
+TENSOR_ADDS = 3
 STORE_GROUPS = (2, 2, 2, 2, 2, 2, 4)
 VECTOR_HELPS = 2
 
@@ -41,11 +42,13 @@ def tile_mora_kernel(tc, x, matrix_words, matrix_scales, out):
         results = ctx.enter_context(tc.tile_pool(name="results", bufs=1))
         psum_t = ctx.enter_context(tc.psum_pool(name="psum_t", bufs=2))
         psum_y = ctx.enter_context(tc.psum_pool(name="psum_y", bufs=4))
+        psum_s = ctx.enter_context(tc.psum_pool(name="psum_s", bufs=2))
         ctx.enter_context(tc.manual_schedule())
 
         w_words = keep.tile([P, PASSES, 2 * RANK], U8, align_bytes=64)
         w_scales = keep.tile([P, PASSES, RANK], U8, align_bytes=64)
         identity = keep.tile([P, P], F32)
+        identity_bf16 = keep.tile([P, P], BF16)
         x_loads = [keep.tile([P, count * HIDDEN], BF16, name="x_load%d" % j) for j, count in enumerate(LOAD_GROUPS)]
         x_sb = []
         for j, count in enumerate(LOAD_GROUPS):
@@ -60,6 +63,7 @@ def tile_mora_kernel(tc, x, matrix_words, matrix_scales, out):
         written = [0 for count in STORE_GROUPS]
 
         nc.vector.memset(w_scales[:].bitcast(I32), 0)
+        make_identity(nc, identity_bf16[:])
         make_identity(nc, identity[:])
 
         def load(j):
@@ -81,17 +85,44 @@ def tile_mora_kernel(tc, x, matrix_words, matrix_scales, out):
             load(j)
 
         turned = {}
+        summed = {}
+
+        def vector_width(i):
+            return K_PASS if i < TENSOR_ADDS else RANK
+
+        def grouped_columns(i):
+            return x_sb[i].rearrange("p (j c) -> p j c", j=GROUPS)
+
+        def tensor_sum(i):
+            total = psum_s.tile([P, RANK - K_PASS], F32, name="total")
+            for j in range(GROUPS):
+                nc.tensor.matmul(
+                    total[:], lhsT=identity_bf16[:], rhs=grouped_columns(i)[:, j, K_PASS:], start=(j == 0), stop=(j == GROUPS - 1)
+                )
+            return total
+
+        def round_tensor_sum(i, total):
+            summed[i] = work.tile([P, RANK], BF16, name="c")
+            nc.scalar.copy(out=summed[i][:, K_PASS:], in_=total[:])
 
         def pair_sums(i):
-            pairs = work.tile([P, 2 * RANK], F32, name="pairs")
+            width = vector_width(i)
+            pairs = work.tile([P, 2, width], F32, name="pairs")
+            columns = grouped_columns(i)
             nc.vector.tensor_tensor(
-                out=pairs[:], in0=x_sb[i][:, : 2 * RANK], in1=x_sb[i][:, 2 * RANK :], op=mybir.AluOpType.add
+                out=pairs[:], in0=columns[:, :2, :width], in1=columns[:, 2:, :width], op=mybir.AluOpType.add
             )
             return pairs
 
-        def finish_sum_and_transpose(i, pairs):
-            c = work.tile([P, RANK], BF16, name="c")
-            nc.vector.tensor_tensor(out=c[:], in0=pairs[:, :RANK], in1=pairs[:, RANK:], op=mybir.AluOpType.add)
+        def finish_sum(i, pairs):
+            if i not in summed:
+                summed[i] = work.tile([P, RANK], BF16, name="c")
+            nc.vector.tensor_tensor(
+                out=summed[i][:, : vector_width(i)], in0=pairs[:, 0, :], in1=pairs[:, 1, :], op=mybir.AluOpType.add
+            )
+
+        def transpose(i):
+            c = summed[i]
             words = c[:].bitcast(F32)
             c_t = psum_t.tile([P, PASSES * HALVES, P], F32, name="c_t")
             for g in range(PASSES):
@@ -135,6 +166,7 @@ def tile_mora_kernel(tc, x, matrix_words, matrix_scales, out):
                 scales=c_scales[:],
                 in_=grouped[:].rearrange("p g r t -> p (g r t)"),
             )
+            halves = []
             for n in range(N_TILES):
                 y = psum_y.tile([P, N_TILE], F32, name="y")
                 for g in range(PASSES):
@@ -147,24 +179,41 @@ def tile_mora_kernel(tc, x, matrix_words, matrix_scales, out):
                         start=(g == 0),
                         stop=(g == PASSES - 1),
                     )
-                if n == N_TILES - 1 and i >= TOKEN_TILES - VECTOR_HELPS:
-                    left_to_vector[i] = y
-                else:
-                    nc.scalar.copy(out=target(i, n), in_=repeated(y))
-                    store_if_full(i, n)
+                halves.append(y)
+            return halves
+
+        def repeat_half(i, n, y):
+            if n == N_TILES - 1 and i >= TOKEN_TILES - VECTOR_HELPS:
+                left_to_vector[i] = y
+            else:
+                nc.scalar.copy(out=target(i, n), in_=repeated(y))
+                store_if_full(i, n)
 
         def vector_helps(i):
             nc.vector.tensor_copy(out=target(i, N_TILES - 1), in_=repeated(left_to_vector[i]))
             store_if_full(i, N_TILES - 1)
 
+        round_tensor_sum(0, tensor_sum(0))
         for i in range(TOKEN_TILES + 2):
             if i < TOKEN_TILES:
                 pairs = pair_sums(i)
             if 1 <= i <= TOKEN_TILES:
                 grouped = regroup(i - 1)
             if i < TOKEN_TILES:
-                finish_sum_and_transpose(i, pairs)
+                finish_sum(i, pairs)
+            if TENSOR_ADDS <= i < TOKEN_TILES:
+                transpose(i)
             if 1 <= i <= TOKEN_TILES:
-                multiply(i - 1, grouped)
+                halves = multiply(i - 1, grouped)
+            if i < TENSOR_ADDS:
+                transpose(i)
+            if i + 1 < TENSOR_ADDS:
+                total = tensor_sum(i + 1)
+            if 1 <= i <= TOKEN_TILES:
+                repeat_half(i - 1, 0, halves[0])
+            if i + 1 < TENSOR_ADDS:
+                round_tensor_sum(i + 1, total)
+            if 1 <= i <= TOKEN_TILES:
+                repeat_half(i - 1, 1, halves[1])
             if i - 2 in left_to_vector:
                 vector_helps(i - 2)

@@ -25,7 +25,7 @@ N_TILES = RANK // N_TILE
 TOKEN_TILES = TOKENS // P
 LOAD_GROUPS = (1, 1, 1, 1, 2, 2)
 TENSOR_ADDS = 3
-STORE_GROUPS = (2, 2, 2, 2, 2, 2, 4)
+STORE_GROUPS = (2, 3, 3, 3, 5)
 VECTOR_HELPS = 2
 
 FLOPS = 2 * TOKENS * RANK * RANK

@@ -45,17 +45,17 @@ def tile_mora_kernel(tc, x, matrix_words, matrix_scales, out):
         psum_s = ctx.enter_context(tc.psum_pool(name="psum_s", bufs=2))
         ctx.enter_context(tc.manual_schedule())
 
-        w_words = keep.tile([P, PASSES, 2 * RANK], U8, align_bytes=64)
+        w_words = keep.tile([P, PASSES, 2 * RANK], U8, align_bytes=256)
         w_scales = keep.tile([P, PASSES, RANK], U8, align_bytes=64)
         identity = keep.tile([P, P], F32)
         identity_bf16 = keep.tile([P, P], BF16)
-        x_loads = [keep.tile([P, count * HIDDEN], BF16, name="x_load%d" % j) for j, count in enumerate(LOAD_GROUPS)]
+        x_loads = [keep.tile([P, count * HIDDEN], BF16, name="x_load%d" % j, align_bytes=256) for j, count in enumerate(LOAD_GROUPS)]
         x_sb = []
         for j, count in enumerate(LOAD_GROUPS):
             for m in range(count):
                 x_sb.append(x_loads[j][:, m * HIDDEN : (m + 1) * HIDDEN])
         HALF = GROUPS * N_TILE
-        out_sb = [results.tile([P, count * HALF], F32, name="out_sb%d" % j) for j, count in enumerate(STORE_GROUPS)]
+        out_sb = [results.tile([P, count * HALF], F32, name="out_sb%d" % j, align_bytes=256) for j, count in enumerate(STORE_GROUPS)]
         place = []
         for j, count in enumerate(STORE_GROUPS):
             for m in range(count):

from contextlib import ExitStack

import concourse.mybir as mybir
from concourse.masks import make_identity

BF16 = mybir.dt.bfloat16
F32 = mybir.dt.float32
I32 = mybir.dt.int32
U32 = mybir.dt.uint32
U8 = mybir.dt.uint8
FP8X4 = mybir.dt.float8_e4m3fn_x4
FP4X4 = mybir.dt.float4_e2m1fn_x4

P = 128
PACK = 4
HALVES = 2
K_PASS = P * PACK
TOKENS = 2 * 512
HIDDEN = 4096
RANK = 1024
GROUPS = HIDDEN // RANK
PASSES = RANK // K_PASS
N_TILE = 512
N_TILES = RANK // N_TILE
TOKEN_TILES = TOKENS // P
LOAD_GROUPS = (1, 1, 1, 1, 2, 2)
TENSOR_ADDS = 3
STORE_GROUPS = (2, 3, 3, 3, 5)
VECTOR_HELPS = 2

FLOPS = 2 * TOKENS * RANK * RANK


def tile_mora_kernel(tc, x, matrix_words, matrix_scales, out):
    nc = tc.nc
    x_rows = x.flatten_outer_dims().rearrange("(p i) h -> p (i h)", i=TOKEN_TILES)
    out_rows = out.flatten_outer_dims().rearrange("(p i) h -> p (i h)", i=TOKEN_TILES)

    with ExitStack() as ctx:
        keep = ctx.enter_context(tc.tile_pool(name="keep", bufs=1))
        work = ctx.enter_context(tc.tile_pool(name="work", bufs=2))
        results = ctx.enter_context(tc.tile_pool(name="results", bufs=1))
        psum_t = ctx.enter_context(tc.psum_pool(name="psum_t", bufs=2))
        psum_y = ctx.enter_context(tc.psum_pool(name="psum_y", bufs=4))
        psum_s = ctx.enter_context(tc.psum_pool(name="psum_s", bufs=2))
        ctx.enter_context(tc.manual_schedule())

        w_words = keep.tile([P, PASSES, 2 * RANK], U8, align_bytes=256)
        w_scales = keep.tile([P, PASSES, RANK], U8, align_bytes=64)
        identity = keep.tile([P, P], F32)
        identity_bf16 = keep.tile([P, P], BF16)
        x_loads = [keep.tile([P, count * HIDDEN], BF16, name="x_load%d" % j, align_bytes=256) for j, count in enumerate(LOAD_GROUPS)]
        x_sb = []
        for j, count in enumerate(LOAD_GROUPS):
            for m in range(count):
                x_sb.append(x_loads[j][:, m * HIDDEN : (m + 1) * HIDDEN])
        HALF = GROUPS * N_TILE
        out_sb = [results.tile([P, count * HALF], F32, name="out_sb%d" % j, align_bytes=256) for j, count in enumerate(STORE_GROUPS)]
        place = []
        for j, count in enumerate(STORE_GROUPS):
            for m in range(count):
                place.append((j, m))
        written = [0 for count in STORE_GROUPS]

        nc.vector.memset(w_scales[:].bitcast(I32), 0)
        make_identity(nc, identity_bf16[:])
        make_identity(nc, identity[:])

        def load(j):
            first = sum(LOAD_GROUPS[:j])
            nc.sync.dma_start(out=x_loads[j][:], in_=x_rows[:, first * HIDDEN : (first + LOAD_GROUPS[j]) * HIDDEN])

        load(0)
        load(1)
        for quadrant in range(4):
            nc.sync.dma_start(
                out=w_scales[32 * quadrant : 32 * quadrant + 4, :, :].bitcast(I32),
                in_=matrix_scales[:, 4 * quadrant : 4 * quadrant + 4, :].bitcast(I32).rearrange("g r w -> r g w"),
            )
        nc.sync.dma_start(
            out=w_words[:].bitcast(I32),
            in_=matrix_words.bitcast(I32).rearrange("g p w -> p g w"),
        )
        for j in range(2, len(LOAD_GROUPS)):
            load(j)

        turned = {}
        summed = {}

        def vector_width(i):
            return K_PASS if i < TENSOR_ADDS else RANK

        def grouped_columns(i):
            return x_sb[i].rearrange("p (j c) -> p j c", j=GROUPS)

        def tensor_sum(i):
            total = psum_s.tile([P, RANK - K_PASS], F32, name="total")
            for j in range(GROUPS):
                nc.tensor.matmul(
                    total[:], lhsT=identity_bf16[:], rhs=grouped_columns(i)[:, j, K_PASS:], start=(j == 0), stop=(j == GROUPS - 1)
                )
            return total

        def round_tensor_sum(i, total):
            summed[i] = work.tile([P, RANK], BF16, name="c")
            nc.scalar.copy(out=summed[i][:, K_PASS:], in_=total[:])

        def pair_sums(i):
            width = vector_width(i)
            pairs = work.tile([P, 2, width], F32, name="pairs")
            columns = grouped_columns(i)
            nc.vector.tensor_tensor(
                out=pairs[:], in0=columns[:, :2, :width], in1=columns[:, 2:, :width], op=mybir.AluOpType.add
            )
            return pairs

        def finish_sum(i, pairs):
            if i not in summed:
                summed[i] = work.tile([P, RANK], BF16, name="c")
            nc.vector.tensor_tensor(
                out=summed[i][:, : vector_width(i)], in0=pairs[:, 0, :], in1=pairs[:, 1, :], op=mybir.AluOpType.add
            )

        def transpose(i):
            c = summed[i]
            words = c[:].bitcast(F32)
            c_t = psum_t.tile([P, PASSES * HALVES, P], F32, name="c_t")
            for g in range(PASSES):
                for u in range(HALVES):
                    nc.tensor.transpose(
                        c_t[:, g * HALVES + u, :],
                        words[:, K_PASS // 2 * g + u : K_PASS // 2 * (g + 1) : HALVES],
                        identity[:],
                    )
            turned[i] = c_t

        def regroup(i):
            grouped = work.tile([P, PASSES, P, PACK], BF16, name="grouped", align_bytes=64)
            nc.vector.tensor_copy(
                out=grouped[:].rearrange("p g r t -> p (g r t)").bitcast(F32).rearrange("p (g r u) -> p g r u", g=PASSES, u=HALVES),
                in_=turned[i][:].rearrange("p (g u) r -> p g r u", g=PASSES),
            )
            return grouped

        def repeated(y):
            return y[:].unsqueeze(2).to_broadcast([P, N_TILE, GROUPS])

        def target(i, n):
            j, m = place[N_TILES * i + n]
            return out_sb[j][:, m * HALF : (m + 1) * HALF].rearrange("p (n j) -> p n j", j=GROUPS)

        def store_if_full(i, n):
            j, m = place[N_TILES * i + n]
            written[j] += 1
            if written[j] == STORE_GROUPS[j]:
                first = sum(STORE_GROUPS[:j])
                nc.sync.dma_start(out=out_rows[:, first * HALF : (first + STORE_GROUPS[j]) * HALF], in_=out_sb[j][:])

        left_to_vector = {}

        def multiply(i, grouped):
            c_codes = work.tile([P, PASSES * P], U32, name="c_codes", align_bytes=64)
            c_scales = work.tile([P, PASSES * P], U8, name="c_scales", align_bytes=64)
            nc.vector.quantize_mx(
                out=c_codes[:].bitcast(FP8X4),
                scales=c_scales[:],
                in_=grouped[:].rearrange("p g r t -> p (g r t)"),
            )
            halves = []
            for n in range(N_TILES):
                y = psum_y.tile([P, N_TILE], F32, name="y")
                for g in range(PASSES):
                    nc.tensor.matmul_mx(
                        out=y[:],
                        lhsT=c_codes[:, g * P : (g + 1) * P].bitcast(FP8X4),
                        lhsT_scale=c_scales[:, g * P : (g + 1) * P],
                        rhs=w_words[:, g, 2 * N_TILE * n : 2 * N_TILE * (n + 1)].bitcast(FP4X4),
                        rhs_scale=w_scales[:, g, N_TILE * n : N_TILE * (n + 1)],
                        start=(g == 0),
                        stop=(g == PASSES - 1),
                    )
                halves.append(y)
            return halves

        def repeat_half(i, n, y):
            if n == N_TILES - 1 and i >= TOKEN_TILES - VECTOR_HELPS:
                left_to_vector[i] = y
            else:
                nc.scalar.copy(out=target(i, n), in_=repeated(y))
                store_if_full(i, n)

        def vector_helps(i):
            nc.vector.tensor_copy(out=target(i, N_TILES - 1), in_=repeated(left_to_vector[i]))
            store_if_full(i, N_TILES - 1)

        round_tensor_sum(0, tensor_sum(0))
        for i in range(TOKEN_TILES + 2):
            if i < TOKEN_TILES:
                pairs = pair_sums(i)
            if 1 <= i <= TOKEN_TILES:
                grouped = regroup(i - 1)
            if i < TOKEN_TILES:
                finish_sum(i, pairs)
            if TENSOR_ADDS <= i < TOKEN_TILES:
                transpose(i)
            if 1 <= i <= TOKEN_TILES:
                halves = multiply(i - 1, grouped)
            if i < TENSOR_ADDS:
                transpose(i)
            if i + 1 < TENSOR_ADDS:
                total = tensor_sum(i + 1)
            if 1 <= i <= TOKEN_TILES:
                repeat_half(i - 1, 0, halves[0])
            if i + 1 < TENSOR_ADDS:
                round_tensor_sum(i + 1, total)
            if 1 <= i <= TOKEN_TILES:
                repeat_half(i - 1, 1, halves[1])
            if i - 2 in left_to_vector:
                vector_helps(i - 2)
